import numpy as np
import ml_dtypes


def mxq(x, axis, fmt="e4m3"):
    dtype, down = {"e4m3": (ml_dtypes.float8_e4m3fn, 7), "e5m2": (ml_dtypes.float8_e5m2, 14)}[fmt]
    v = np.moveaxis(np.asarray(x, np.float32).astype(ml_dtypes.bfloat16).astype(np.float64), axis, -1)
    blocks = v.reshape(v.shape[:-1] + (-1, 32))
    amax = np.abs(blocks).max(-1, keepdims=True)
    byte = np.maximum(np.where(amax > 0, np.frexp(amax)[1] - 1 + 127, 0) - down, 1)
    scale = np.exp2(byte - 127.0)
    codes = (blocks / scale).astype(np.float32).astype(dtype).astype(np.float64)
    return np.moveaxis((codes * scale).reshape(v.shape), -1, axis)


WIDE = False


def mx_kscale(k):
    if not WIDE:
        return np.ones(k)
    levels = np.array([10, -10, 5, -5, 0])
    a = np.random.permutation(np.resize(levels, k // 512 * 4)).reshape(k // 512, 4)
    idx = np.arange(k)
    return np.exp2(a[idx // 512, idx % 128 // 32])


BF16 = ml_dtypes.bfloat16


def bf(x):
    return np.asarray(x, np.float32).astype(BF16)


def f64(x):
    return np.asarray(x).astype(np.float64)


B, S, E, H, W = 64, 64, 512, 8, 16


def setup_inputs():
    s = mx_kscale(E)
    t = mx_kscale(2 * E)
    th, tv = t[:E], t[E:]
    return {
        "h_ctx": bf(np.random.standard_normal((B, S, E)) * 0.35 * s),
        "v_ctx": bf(np.random.standard_normal((B, S, E)) * 0.35 * s),
        "h_out_w": bf(np.random.standard_normal((E, E)) * 2.5 / np.sqrt(E) / s[None, :] * th[:, None]),
        "h_out_b": bf(np.random.standard_normal(E) * 0.2 * th),
        "v_out_w": bf(np.random.standard_normal((E, E)) * 2.5 / np.sqrt(E) / s[None, :] * tv[:, None]),
        "v_out_b": bf(np.random.standard_normal(E) * 0.2 * tv),
        "mlp_w1": bf(np.random.standard_normal((E, 2 * E)) / np.sqrt(2 * E) / t[None, :]),
        "mlp_b1": bf(np.random.standard_normal(E) * 0.2),
    }


def reference(h_ctx, v_ctx, h_out_w, h_out_b, v_out_w, v_out_b, mlp_w1, mlp_b1):
    h_out = (mxq(f64(h_ctx), 2, "e4m3") @ mxq(f64(h_out_w), 1, "e4m3").T) + f64(h_out_b)
    v_out = (mxq(f64(v_ctx), 2, "e4m3") @ mxq(f64(v_out_w), 1, "e4m3").T) + f64(v_out_b)
    combined = np.concatenate([h_out, v_out], axis=-1)
    return np.maximum((mxq(combined, 2, "e4m3") @ mxq(f64(mlp_w1), 1, "e4m3").T) + f64(mlp_b1), 0.0)

@@ -1,0 +1,257 @@
+from contextlib import ExitStack
+
+import concourse.mybir as mybir
+from concourse.masks import make_identity
+
+F32 = mybir.dt.float32
+BF16 = mybir.dt.bfloat16
+U32 = mybir.dt.uint32
+U8 = mybir.dt.uint8
+FP8X4 = mybir.dt.float8_e4m3fn_x4
+ACT = mybir.ActivationFunctionType
+ALU = mybir.AluOpType
+
+P = 128
+E = 512
+CHUNK = 512
+N_CHUNKS = 8
+N_UNITS = 2 * N_CHUNKS
+FLOPS = 2 * 4096 * 512 * 512 * 2 + 2 * 4096 * 1024 * 512
+
+PINNED = False
+XT_V_BELOW = 2
+X1_V_BELOW = 2
+RELU_S_FROM = 6
+RELU_S_TILES = 1
+S2_LAG = 3
+
+
+def tile_bispa_pa_t_kernel(
+    tc, h_ctx, v_ctx, h_out_w, h_out_b, v_out_w, v_out_b, mlp_w1, mlp_b1, out
+):
+    nc = tc.nc
+    with ExitStack() as ctx:
+        consts = ctx.enter_context(tc.tile_pool(name="consts", bufs=1))
+        raw = ctx.enter_context(tc.tile_pool(name="raw", bufs=1))
+        wq = ctx.enter_context(tc.tile_pool(name="wq", bufs=1))
+        grp_pool = ctx.enter_context(tc.tile_pool(name="grp", bufs=3))
+        xq = ctx.enter_context(tc.tile_pool(name="xq", bufs=4))
+        pl_pool = ctx.enter_context(tc.tile_pool(name="pl", bufs=3))
+        g2_pool = ctx.enter_context(tc.tile_pool(name="g2", bufs=3))
+        cq = ctx.enter_context(tc.tile_pool(name="cq", bufs=6))
+        ob_pool = ctx.enter_context(tc.tile_pool(name="ob", bufs=3))
+        ps_tp = ctx.enter_context(tc.psum_pool(name="ps_tp", bufs=2))
+        ps_s1 = ctx.enter_context(tc.psum_pool(name="ps_s1", bufs=4))
+        ps_s2 = ctx.enter_context(tc.psum_pool(name="ps_s2", bufs=2))
+        if PINNED:
+            ctx.enter_context(tc.manual_schedule())
+
+        hx = h_ctx.flatten_outer_dims()
+        vx = v_ctx.flatten_outer_dims()
+        of = out.flatten_outer_dims()
+
+        zb = consts.tile([P, 2 * P], BF16, name="zb")
+        nc.vector.memset(zb[:], 0.0)
+        zrow = consts.tile([P, E], BF16, name="zrow")
+        nc.vector.memset(zrow[:], 0.0)
+        ones = consts.tile([P, P], BF16, name="ones")
+        nc.vector.memset(ones[:], 1.0)
+        ident = consts.tile([P, P], F32, name="ident")
+        make_identity(nc, ident[:])
+        nc.scalar.dma_start(out=zb[0:2, :], in_=h_out_b.rearrange("(u w) -> u w", u=2))
+        nc.scalar.dma_start(out=zb[2:4, :], in_=v_out_b.rearrange("(u w) -> u w", u=2))
+        nc.scalar.dma_start(out=zrow[0:1, :], in_=mlp_b1.rearrange("(o n) -> o n", o=1))
+
+        def load_proj(w, name):
+            t = raw.tile([P, 4 * E], BF16, name=name)
+            nc.sync.dma_start(
+                out=t[:].rearrange("q (u e k) -> q u e k", u=2, e=2),
+                in_=w.rearrange("(u q e) k -> q u e k", u=2, e=2),
+            )
+            return t
+
+        def load_ctx(x, c, name):
+            t = raw.tile([P, 4 * E], BF16, name=name)
+            nc.sync.dma_start(
+                out=t[:].rearrange("p (a k) -> p a k", a=4),
+                in_=x[c * CHUNK : (c + 1) * CHUNK, :].rearrange("(p a) k -> p a k", a=4),
+            )
+            return t
+
+        ctx_raw = {}
+        hw_raw = load_proj(h_out_w, "hw_raw")
+        ctx_raw[0] = load_ctx(hx, 0, "x0")
+        vw_raw = load_proj(v_out_w, "vw_raw")
+        ctx_raw[1] = load_ctx(vx, 0, "x1")
+        w1_raw = raw.tile([P, 4 * 2 * E], BF16, name="w1_raw")
+        nc.sync.dma_start(
+            out=w1_raw[:].rearrange("p (j k) -> p j k", j=4),
+            in_=mlp_w1.rearrange("(j p) k -> p j k", p=P),
+        )
+        for c in range(1, N_CHUNKS):
+            ctx_raw[2 * c] = load_ctx(hx, c, "x%d" % (2 * c))
+            ctx_raw[2 * c + 1] = load_ctx(vx, c, "x%d" % (2 * c + 1))
+
+        def copy_out(on_vector, dst, src):
+            if on_vector:
+                nc.vector.tensor_copy(out=dst, in_=src)
+            else:
+                nc.scalar.copy(out=dst, in_=src)
+
+        def transpose_quantise(words, row_words, first_word, codes, scales, second_on_vector):
+            grp = grp_pool.tile([P, 4 * E], BF16, align_bytes=64)
+            grp_words = grp[:].bitcast(F32)
+            for half in range(2):
+                bank = ps_tp.tile([P, E], F32, tag="tp")
+                for jj in range(2):
+                    for u in range(2):
+                        start = (2 * half + jj) * row_words + first_word + u * P
+                        nc.tensor.transpose(
+                            bank[:, u * 256 + jj * P : u * 256 + (jj + 1) * P],
+                            words[:, start : start + P],
+                            ident[:],
+                        )
+                copy_out(
+                    second_on_vector and half == 1,
+                    grp_words[:, half * E : (half + 1) * E].rearrange("p (r u) -> p r u", u=2),
+                    bank[:].rearrange("p (u r) -> p r u", u=2),
+                )
+            nc.vector.quantize_mx(out=codes[:].bitcast(FP8X4), scales=scales[:], in_=grp[:])
+
+        def weight_unit(words, row_words, first_word, name, second_on_vector):
+            codes = wq.tile([P, E], U32, name=name + "_c", align_bytes=64)
+            scales = wq.tile([P, E], U8, name=name + "_s", align_bytes=64)
+            transpose_quantise(words, row_words, first_word, codes, scales, second_on_vector)
+            return codes, scales
+
+        state = {}
+
+        def prepare_biases():
+            bank = ps_tp.tile([P, E], F32, tag="tp")
+            nc.tensor.transpose(bank[:, 0:P], zb[:].bitcast(F32), ident[:])
+            bias8 = consts.tile([P, 8], F32, name="bias8")
+            nc.vector.tensor_copy(out=bias8[:], in_=bank[:].bitcast(BF16)[:, 0:8])
+            state["bias8"] = bias8
+            acc = ps_s2.tile([P, E], F32, tag="s2")
+            nc.tensor.matmul(out=acc[:], lhsT=ones[:], rhs=zrow[:], start=True, stop=True)
+            b1_bc = consts.tile([P, E], F32, name="b1_bc")
+            nc.vector.tensor_copy(out=b1_bc[:], in_=acc[:])
+            state["b1_bc"] = b1_bc
+
+        def tq(j):
+            if j < 0 or j >= N_UNITS:
+                return
+            if j == 0:
+                state["w0"] = weight_unit(hw_raw[:].bitcast(F32), 256, 0, "hw", True)
+            if j == 1:
+                state["w1"] = weight_unit(vw_raw[:].bitcast(F32), 256, 0, "vw", True)
+            xc = xq.tile([P, E], U32, align_bytes=64)
+            xs = xq.tile([P, E], U8, align_bytes=64)
+            transpose_quantise(ctx_raw[j][:].bitcast(F32), 256, 0, xc, xs, j < XT_V_BELOW)
+            state["x%d" % j] = (xc, xs)
+            if j == 0:
+                prepare_biases()
+            if j == 1:
+                state["m0"] = weight_unit(w1_raw[:].bitcast(F32), 512, 0, "w1a", False)
+            if j == 2:
+                state["m1"] = weight_unit(w1_raw[:].bitcast(F32), 512, 256, "w1b", False)
+
+        def stage1(j):
+            if j < 0 or j >= N_UNITS:
+                return
+            s = j % 2
+            wc, ws = state["w%d" % s]
+            xc, xs = state["x%d" % j]
+            bias8 = state["bias8"]
+            planar = pl_pool.tile([P, 4 * CHUNK], BF16)
+            banks = []
+            for t in range(4):
+                acc1 = ps_s1.tile([P, CHUNK], F32, tag="s1")
+                nc.tensor.matmul_mx(
+                    out=acc1[:],
+                    lhsT=wc[:, t * P : (t + 1) * P].bitcast(FP8X4),
+                    lhsT_scale=ws[:, t * P : (t + 1) * P],
+                    rhs=xc[:].bitcast(FP8X4),
+                    rhs_scale=xs[:],
+                    start=True,
+                    stop=True,
+                )
+                banks.append(acc1)
+            for t in range(4):
+                dst = planar[:, t * CHUNK : (t + 1) * CHUNK]
+                b = bias8[:, 4 * s + t : 4 * s + t + 1]
+                if j < X1_V_BELOW and t % 2 == 1:
+                    nc.vector.tensor_scalar_add(out=dst, in0=banks[t][:], scalar1=b)
+                else:
+                    nc.scalar.activation(out=dst, in_=banks[t][:], func=ACT.Identity, bias=b, scale=1.0)
+            state["p%d" % j] = planar
+
+        def regroup(j):
+            if j < 0 or j >= N_UNITS:
+                return
+            planar = state["p%d" % j]
+            g2 = g2_pool.tile([P, 4 * CHUNK], BF16, align_bytes=64)
+            nc.vector.tensor_copy(
+                out=g2[:].rearrange("p (c i t) -> p c t i", i=4, t=4),
+                in_=planar[:].rearrange("p (t c i) -> p c t i", t=4, i=4),
+            )
+            state["g%d" % j] = g2
+
+        def quantise2(j):
+            if j < 0 or j >= N_UNITS:
+                return
+            cc = cq.tile([P, CHUNK], U32, align_bytes=64)
+            cs = cq.tile([P, CHUNK], U8, align_bytes=64)
+            nc.vector.quantize_mx(out=cc[:].bitcast(FP8X4), scales=cs[:], in_=state["g%d" % j][:])
+            state["c%d" % j] = (cc, cs)
+
+        def stage2(q):
+            if q < 0 or q >= N_UNITS:
+                return
+            c = q // 2
+            if q % 2 == 0:
+                ob = ob_pool.tile([P, 4 * E], F32)
+                state["ob"] = ob
+            ob = state["ob"]
+            b1_bc = state["b1_bc"]
+            tiles = (0, 1) if q % 2 == 0 else (2, 3)
+            banks = []
+            for a in tiles:
+                acc2 = ps_s2.tile([P, E], F32, tag="s2")
+                for g in range(2):
+                    cc, cs = state["c%d" % (2 * c + g)]
+                    mc, ms = state["m%d" % g]
+                    nc.tensor.matmul_mx(
+                        out=acc2[:],
+                        lhsT=cc[:, a * P : (a + 1) * P].bitcast(FP8X4),
+                        lhsT_scale=cs[:, a * P : (a + 1) * P],
+                        rhs=mc[:].bitcast(FP8X4),
+                        rhs_scale=ms[:],
+                        start=(g == 0),
+                        stop=(g == 1),
+                    )
+                banks.append(acc2)
+            for a, acc2 in zip(tiles, banks):
+                nc.vector.tensor_tensor(
+                    out=ob[:, a * E : (a + 1) * E], in0=acc2[:], in1=b1_bc[:], op=ALU.add
+                )
+            on_scalar = [a for a in tiles if c >= RELU_S_FROM or a >= 4 - RELU_S_TILES]
+            on_vector = [a for a in tiles if a not in on_scalar]
+            if on_vector:
+                span = ob[:, on_vector[0] * E : (on_vector[-1] + 1) * E]
+                nc.vector.tensor_scalar_max(out=span, in0=span, scalar1=0.0)
+            for a in on_scalar:
+                span = ob[:, a * E : (a + 1) * E]
+                nc.scalar.activation(out=span, in_=span, func=ACT.Relu)
+            if q % 2 == 1:
+                nc.sync.dma_start(
+                    out=of[c * CHUNK : (c + 1) * CHUNK, :].rearrange("(p a) f -> p a f", a=4),
+                    in_=ob[:].rearrange("p (a f) -> p a f", a=4),
+                )
+
+        for m in range(-1, N_UNITS + S2_LAG):
+            tq(m + 1)
+            stage1(m)
+            stage2(m - S2_LAG)
+            regroup(m)
+            quantise2(m)

@@ -23,7 +23,7 @@ XT_V_BELOW = 2
 X1_V_BELOW = 2
 RELU_S_FROM = 6
 RELU_S_TILES = 1
-S2_LAG = 3
+S2_LAG = 2
 
 
 def tile_bispa_pa_t_kernel(
@@ -39,7 +39,7 @@ def tile_bispa_pa_t_kernel(
         pl_pool = ctx.enter_context(tc.tile_pool(name="pl", bufs=3))
         g2_pool = ctx.enter_context(tc.tile_pool(name="g2", bufs=3))
         cq = ctx.enter_context(tc.tile_pool(name="cq", bufs=6))
-        ob_pool = ctx.enter_context(tc.tile_pool(name="ob", bufs=3))
+        ob_pool = ctx.enter_context(tc.tile_pool(name="ob", bufs=4))
         ps_tp = ctx.enter_context(tc.psum_pool(name="ps_tp", bufs=2))
         ps_s1 = ctx.enter_context(tc.psum_pool(name="ps_s1", bufs=4))
         ps_s2 = ctx.enter_context(tc.psum_pool(name="ps_s2", bufs=2))
@@ -58,9 +58,9 @@ def tile_bispa_pa_t_kernel(
         nc.vector.memset(ones[:], 1.0)
         ident = consts.tile([P, P], F32, name="ident")
         make_identity(nc, ident[:])
-        nc.scalar.dma_start(out=zb[0:2, :], in_=h_out_b.rearrange("(u w) -> u w", u=2))
-        nc.scalar.dma_start(out=zb[2:4, :], in_=v_out_b.rearrange("(u w) -> u w", u=2))
-        nc.scalar.dma_start(out=zrow[0:1, :], in_=mlp_b1.rearrange("(o n) -> o n", o=1))
+        nc.sync.dma_start(out=zb[0:2, :], in_=h_out_b.rearrange("(u w) -> u w", u=2))
+        nc.sync.dma_start(out=zb[2:4, :], in_=v_out_b.rearrange("(u w) -> u w", u=2))
+        nc.sync.dma_start(out=zrow[0:1, :], in_=mlp_b1.rearrange("(o n) -> o n", o=1))
 
         def load_proj(w, name):
             t = raw.tile([P, 4 * E], BF16, name=name)
@@ -141,20 +141,10 @@ def tile_bispa_pa_t_kernel(
         def tq(j):
             if j < 0 or j >= N_UNITS:
                 return
-            if j == 0:
-                state["w0"] = weight_unit(hw_raw[:].bitcast(F32), 256, 0, "hw", True)
-            if j == 1:
-                state["w1"] = weight_unit(vw_raw[:].bitcast(F32), 256, 0, "vw", True)
             xc = xq.tile([P, E], U32, align_bytes=64)
             xs = xq.tile([P, E], U8, align_bytes=64)
             transpose_quantise(ctx_raw[j][:].bitcast(F32), 256, 0, xc, xs, j < XT_V_BELOW)
             state["x%d" % j] = (xc, xs)
-            if j == 0:
-                prepare_biases()
-            if j == 1:
-                state["m0"] = weight_unit(w1_raw[:].bitcast(F32), 512, 0, "w1a", False)
-            if j == 2:
-                state["m1"] = weight_unit(w1_raw[:].bitcast(F32), 512, 256, "w1b", False)
 
         def stage1(j):
             if j < 0 or j >= N_UNITS:
@@ -205,18 +195,21 @@ def tile_bispa_pa_t_kernel(
             nc.vector.quantize_mx(out=cc[:].bitcast(FP8X4), scales=cs[:], in_=state["g%d" % j][:])
             state["c%d" % j] = (cc, cs)
 
+        def relu_tiles(q, on_scalar):
+            c = q // 2
+            tiles = (0, 1) if q % 2 == 0 else (2, 3)
+            return [a - tiles[0] for a in tiles if (c >= RELU_S_FROM or a >= 4 - RELU_S_TILES) == on_scalar]
+
         def stage2(q):
             if q < 0 or q >= N_UNITS:
                 return
             c = q // 2
-            if q % 2 == 0:
-                ob = ob_pool.tile([P, 4 * E], F32)
-                state["ob"] = ob
-            ob = state["ob"]
+            ob = ob_pool.tile([P, 2 * E], F32)
+            state["o%d" % q] = ob
             b1_bc = state["b1_bc"]
-            tiles = (0, 1) if q % 2 == 0 else (2, 3)
             banks = []
-            for a in tiles:
+            for i in range(2):
+                a = 2 * (q % 2) + i
                 acc2 = ps_s2.tile([P, E], F32, tag="s2")
                 for g in range(2):
                     cc, cs = state["c%d" % (2 * c + g)]
@@ -231,27 +224,47 @@ def tile_bispa_pa_t_kernel(
                         stop=(g == 1),
                     )
                 banks.append(acc2)
-            for a, acc2 in zip(tiles, banks):
+            for i in range(2):
                 nc.vector.tensor_tensor(
-                    out=ob[:, a * E : (a + 1) * E], in0=acc2[:], in1=b1_bc[:], op=ALU.add
-                )
-            on_scalar = [a for a in tiles if c >= RELU_S_FROM or a >= 4 - RELU_S_TILES]
-            on_vector = [a for a in tiles if a not in on_scalar]
-            if on_vector:
-                span = ob[:, on_vector[0] * E : (on_vector[-1] + 1) * E]
-                nc.vector.tensor_scalar_max(out=span, in0=span, scalar1=0.0)
-            for a in on_scalar:
-                span = ob[:, a * E : (a + 1) * E]
-                nc.scalar.activation(out=span, in_=span, func=ACT.Relu)
-            if q % 2 == 1:
-                nc.sync.dma_start(
-                    out=of[c * CHUNK : (c + 1) * CHUNK, :].rearrange("(p a) f -> p a f", a=4),
-                    in_=ob[:].rearrange("p (a f) -> p a f", a=4),
+                    out=ob[:, i * E : (i + 1) * E], in0=banks[i][:], in1=b1_bc[:], op=ALU.add
                 )
 
-        for m in range(-1, N_UNITS + S2_LAG):
-            tq(m + 1)
+        def relu_vector(q):
+            if q < 0 or q >= N_UNITS:
+                return
+            mine = relu_tiles(q, False)
+            if mine:
+                span = state["o%d" % q][:, mine[0] * E : (mine[-1] + 1) * E]
+                nc.vector.tensor_scalar_max(out=span, in0=span, scalar1=0.0)
+
+        def relu_scalar_and_store(q):
+            if q < 0 or q >= N_UNITS:
+                return
+            c = q // 2
+            ob = state["o%d" % q]
+            for i in relu_tiles(q, True):
+                span = ob[:, i * E : (i + 1) * E]
+                nc.scalar.activation(out=span, in_=span, func=ACT.Relu)
+            rows = of[c * CHUNK : (c + 1) * CHUNK, :].rearrange("(p a) f -> p a f", a=4)
+            first = 2 * (q % 2)
+            nc.sync.dma_start(
+                out=rows[:, first : first + 2, :], in_=ob[:].rearrange("p (a f) -> p a f", a=2)
+            )
+
+        prepare_biases()
+        state["w0"] = weight_unit(hw_raw[:].bitcast(F32), 256, 0, "hw", True)
+        tq(0)
+        state["w1"] = weight_unit(vw_raw[:].bitcast(F32), 256, 0, "vw", True)
+        tq(1)
+        for m in range(N_UNITS + S2_LAG + 1):
             stage1(m)
-            stage2(m - S2_LAG)
             regroup(m)
+            if m == 0:
+                state["m0"] = weight_unit(w1_raw[:].bitcast(F32), 512, 0, "w1a", False)
+            if m == 1:
+                state["m1"] = weight_unit(w1_raw[:].bitcast(F32), 512, 256, "w1b", False)
+            tq(m + 2)
             quantise2(m)
+            relu_scalar_and_store(m - S2_LAG - 1)
+            stage2(m - S2_LAG)
+            relu_vector(m - S2_LAG)

@@ -22,7 +22,7 @@ PINNED = False
 XT_V_BELOW = 2
 X1_V_BELOW = 2
 RELU_S_FROM = 6
-RELU_S_TILES = 1
+RELU_S_TILES = 2
 S2_LAG = 2
 
 
@@ -40,9 +40,9 @@ def tile_bispa_pa_t_kernel(
         g2_pool = ctx.enter_context(tc.tile_pool(name="g2", bufs=3))
         cq = ctx.enter_context(tc.tile_pool(name="cq", bufs=6))
         ob_pool = ctx.enter_context(tc.tile_pool(name="ob", bufs=4))
-        ps_tp = ctx.enter_context(tc.psum_pool(name="ps_tp", bufs=2))
-        ps_s1 = ctx.enter_context(tc.psum_pool(name="ps_s1", bufs=4))
-        ps_s2 = ctx.enter_context(tc.psum_pool(name="ps_s2", bufs=2))
+        ps_tp = ctx.enter_context(tc.psum_pool(name="ps", bufs=8))
+        ps_s1 = ps_tp
+        ps_s2 = ps_tp
         if PINNED:
             ctx.enter_context(tc.manual_schedule())
 
@@ -102,7 +102,7 @@ def tile_bispa_pa_t_kernel(
             grp = grp_pool.tile([P, 4 * E], BF16, align_bytes=64)
             grp_words = grp[:].bitcast(F32)
             for half in range(2):
-                bank = ps_tp.tile([P, E], F32, tag="tp")
+                bank = ps_tp.tile([P, E], F32, tag="ps")
                 for jj in range(2):
                     for u in range(2):
                         start = (2 * half + jj) * row_words + first_word + u * P
@@ -127,12 +127,12 @@ def tile_bispa_pa_t_kernel(
         state = {}
 
         def prepare_biases():
-            bank = ps_tp.tile([P, E], F32, tag="tp")
+            bank = ps_tp.tile([P, E], F32, tag="ps")
             nc.tensor.transpose(bank[:, 0:P], zb[:].bitcast(F32), ident[:])
             bias8 = consts.tile([P, 8], F32, name="bias8")
             nc.vector.tensor_copy(out=bias8[:], in_=bank[:].bitcast(BF16)[:, 0:8])
             state["bias8"] = bias8
-            acc = ps_s2.tile([P, E], F32, tag="s2")
+            acc = ps_s2.tile([P, E], F32, tag="ps")
             nc.tensor.matmul(out=acc[:], lhsT=ones[:], rhs=zrow[:], start=True, stop=True)
             b1_bc = consts.tile([P, E], F32, name="b1_bc")
             nc.vector.tensor_copy(out=b1_bc[:], in_=acc[:])
@@ -156,7 +156,7 @@ def tile_bispa_pa_t_kernel(
             planar = pl_pool.tile([P, 4 * CHUNK], BF16)
             banks = []
             for t in range(4):
-                acc1 = ps_s1.tile([P, CHUNK], F32, tag="s1")
+                acc1 = ps_s1.tile([P, CHUNK], F32, tag="ps")
                 nc.tensor.matmul_mx(
                     out=acc1[:],
                     lhsT=wc[:, t * P : (t + 1) * P].bitcast(FP8X4),
@@ -210,7 +210,7 @@ def tile_bispa_pa_t_kernel(
             banks = []
             for i in range(2):
                 a = 2 * (q % 2) + i
-                acc2 = ps_s2.tile([P, E], F32, tag="s2")
+                acc2 = ps_s2.tile([P, E], F32, tag="ps")
                 for g in range(2):
                     cc, cs = state["c%d" % (2 * c + g)]
                     mc, ms = state["m%d" % g]

@@ -232,7 +232,7 @@ def tile_bispa_pa_t_kernel(
         def relu_vector(q):
             if q < 0 or q >= N_UNITS:
                 return
-            mine = relu_tiles(q, False)
+            mine = []
             if mine:
                 span = state["o%d" % q][:, mine[0] * E : (mine[-1] + 1) * E]
                 nc.vector.tensor_scalar_max(out=span, in0=span, scalar1=0.0)
@@ -242,14 +242,17 @@ def tile_bispa_pa_t_kernel(
                 return
             c = q // 2
             ob = state["o%d" % q]
-            for i in relu_tiles(q, True):
-                span = ob[:, i * E : (i + 1) * E]
-                nc.scalar.activation(out=span, in_=span, func=ACT.Relu)
             rows = of[c * CHUNK : (c + 1) * CHUNK, :].rearrange("(p a) f -> p a f", a=4)
             first = 2 * (q % 2)
-            nc.sync.dma_start(
-                out=rows[:, first : first + 2, :], in_=ob[:].rearrange("p (a f) -> p a f", a=2)
-            )
+            for i in range(2):
+                span = ob[:, i * E : (i + 1) * E]
+                if c >= RELU_S_FROM:
+                    nc.scalar.activation(out=span, in_=span, func=ACT.Relu)
+                else:
+                    nc.gpsimd.tensor_scalar(
+                        out=span, in0=span, scalar1=1.0, scalar2=0.0, op0=ALU.mult, op1=ALU.max
+                    )
+                nc.sync.dma_start(out=rows[:, first + i, :], in_=span)
 
         prepare_biases()
         state["w0"] = weight_unit(hw_raw[:].bitcast(F32), 256, 0, "hw", True)

@@ -232,7 +232,7 @@ def tile_bispa_pa_t_kernel(
         def relu_vector(q):
             if q < 0 or q >= N_UNITS:
                 return
-            mine = []
+            mine = relu_tiles(q, False)
             if mine:
                 span = state["o%d" % q][:, mine[0] * E : (mine[-1] + 1) * E]
                 nc.vector.tensor_scalar_max(out=span, in0=span, scalar1=0.0)
@@ -244,15 +244,16 @@ def tile_bispa_pa_t_kernel(
             ob = state["o%d" % q]
             rows = of[c * CHUNK : (c + 1) * CHUNK, :].rearrange("(p a) f -> p a f", a=4)
             first = 2 * (q % 2)
-            for i in range(2):
+            mine = relu_tiles(q, True)
+            for i in mine:
                 span = ob[:, i * E : (i + 1) * E]
-                if c >= RELU_S_FROM:
-                    nc.scalar.activation(out=span, in_=span, func=ACT.Relu)
-                else:
-                    nc.gpsimd.tensor_scalar(
-                        out=span, in0=span, scalar1=1.0, scalar2=0.0, op0=ALU.mult, op1=ALU.max
-                    )
-                nc.sync.dma_start(out=rows[:, first + i, :], in_=span)
+                nc.scalar.activation(out=span, in_=span, func=ACT.Relu)
+                if len(mine) == 2:
+                    nc.sync.dma_start(out=rows[:, first + i, :], in_=span)
+            if len(mine) < 2:
+                nc.sync.dma_start(
+                    out=rows[:, first : first + 2, :], in_=ob[:].rearrange("p (a f) -> p a f", a=2)
+                )
 
         prepare_biases()
         state["w0"] = weight_unit(hw_raw[:].bitcast(F32), 256, 0, "hw", True)

@@ -18,7 +18,7 @@ N_CHUNKS = 8
 N_UNITS = 2 * N_CHUNKS
 FLOPS = 2 * 4096 * 512 * 512 * 2 + 2 * 4096 * 1024 * 512
 
-PINNED = False
+PINNED = True
 XT_V_BELOW = 2
 X1_V_BELOW = 2
 RELU_S_FROM = 6
@@ -35,10 +35,10 @@ def tile_bispa_pa_t_kernel(
         raw = ctx.enter_context(tc.tile_pool(name="raw", bufs=1))
         wq = ctx.enter_context(tc.tile_pool(name="wq", bufs=1))
         grp_pool = ctx.enter_context(tc.tile_pool(name="grp", bufs=3))
-        xq = ctx.enter_context(tc.tile_pool(name="xq", bufs=4))
+        xq = ctx.enter_context(tc.tile_pool(name="xq", bufs=5))
         pl_pool = ctx.enter_context(tc.tile_pool(name="pl", bufs=3))
         g2_pool = ctx.enter_context(tc.tile_pool(name="g2", bufs=3))
-        cq = ctx.enter_context(tc.tile_pool(name="cq", bufs=6))
+        cq = ctx.enter_context(tc.tile_pool(name="cq", bufs=7))
         ob_pool = ctx.enter_context(tc.tile_pool(name="ob", bufs=4))
         ps_tp = ctx.enter_context(tc.psum_pool(name="ps", bufs=8))
         ps_s1 = ps_tp
@@ -92,15 +92,13 @@ def tile_bispa_pa_t_kernel(
             ctx_raw[2 * c] = load_ctx(hx, c, "x%d" % (2 * c))
             ctx_raw[2 * c + 1] = load_ctx(vx, c, "x%d" % (2 * c + 1))
 
-        def copy_out(on_vector, dst, src):
-            if on_vector:
-                nc.vector.tensor_copy(out=dst, in_=src)
-            else:
-                nc.scalar.copy(out=dst, in_=src)
+        state = {}
 
-        def transpose_quantise(words, row_words, first_word, codes, scales, second_on_vector):
-            grp = grp_pool.tile([P, 4 * E], BF16, align_bytes=64)
-            grp_words = grp[:].bitcast(F32)
+        def in_range(j):
+            return 0 <= j < N_UNITS
+
+        def transposes(key, words, row_words, first_word):
+            banks = []
             for half in range(2):
                 bank = ps_tp.tile([P, E], F32, tag="ps")
                 for jj in range(2):
@@ -111,20 +109,57 @@ def tile_bispa_pa_t_kernel(
                             words[:, start : start + P],
                             ident[:],
                         )
-                copy_out(
-                    second_on_vector and half == 1,
-                    grp_words[:, half * E : (half + 1) * E].rearrange("p (r u) -> p r u", u=2),
-                    bank[:].rearrange("p (u r) -> p r u", u=2),
-                )
-            nc.vector.quantize_mx(out=codes[:].bitcast(FP8X4), scales=scales[:], in_=grp[:])
+                banks.append(bank)
+            state["tb" + key] = banks
 
-        def weight_unit(words, row_words, first_word, name, second_on_vector):
-            codes = wq.tile([P, E], U32, name=name + "_c", align_bytes=64)
-            scales = wq.tile([P, E], U8, name=name + "_s", align_bytes=64)
-            transpose_quantise(words, row_words, first_word, codes, scales, second_on_vector)
-            return codes, scales
+        def copies_out(key, second_on_vector):
+            grp = grp_pool.tile([P, 4 * E], BF16, align_bytes=64)
+            grp_words = grp[:].bitcast(F32)
+            for half in range(2):
+                dst = grp_words[:, half * E : (half + 1) * E].rearrange("p (r u) -> p r u", u=2)
+                src = state["tb" + key][half][:].rearrange("p (u r) -> p r u", u=2)
+                if second_on_vector and half == 1:
+                    nc.vector.tensor_copy(out=dst, in_=src)
+                else:
+                    nc.scalar.copy(out=dst, in_=src)
+            state["gr" + key] = grp
 
-        state = {}
+        def quantise(key, codes, scales):
+            nc.vector.quantize_mx(out=codes[:].bitcast(FP8X4), scales=scales[:], in_=state["gr" + key][:])
+            state[key] = (codes, scales)
+
+        WEIGHTS = {
+            "w0": (hw_raw, 256, 0, True),
+            "w1": (vw_raw, 256, 0, True),
+            "m0": (w1_raw, 512, 0, False),
+            "m1": (w1_raw, 512, 256, False),
+        }
+
+        def w_transposes(key):
+            tile_, row_words, first_word, on_v = WEIGHTS[key]
+            transposes(key, tile_[:].bitcast(F32), row_words, first_word)
+
+        def w_copies(key):
+            copies_out(key, WEIGHTS[key][3])
+
+        def w_quantise(key):
+            codes = wq.tile([P, E], U32, name=key + "_c", align_bytes=64)
+            scales = wq.tile([P, E], U8, name=key + "_s", align_bytes=64)
+            quantise(key, codes, scales)
+
+        def x_transposes(j):
+            if in_range(j):
+                transposes("x%d" % j, ctx_raw[j][:].bitcast(F32), 256, 0)
+
+        def x_copies(j):
+            if in_range(j):
+                copies_out("x%d" % j, j < XT_V_BELOW)
+
+        def x_quantise(j):
+            if in_range(j):
+                xc = xq.tile([P, E], U32, align_bytes=64)
+                xs = xq.tile([P, E], U8, align_bytes=64)
+                quantise("x%d" % j, xc, xs)
 
         def prepare_biases():
             bank = ps_tp.tile([P, E], F32, tag="ps")
@@ -138,22 +173,11 @@ def tile_bispa_pa_t_kernel(
             nc.vector.tensor_copy(out=b1_bc[:], in_=acc[:])
             state["b1_bc"] = b1_bc
 
-        def tq(j):
-            if j < 0 or j >= N_UNITS:
+        def s1_passes(j):
+            if not in_range(j):
                 return
-            xc = xq.tile([P, E], U32, align_bytes=64)
-            xs = xq.tile([P, E], U8, align_bytes=64)
-            transpose_quantise(ctx_raw[j][:].bitcast(F32), 256, 0, xc, xs, j < XT_V_BELOW)
-            state["x%d" % j] = (xc, xs)
-
-        def stage1(j):
-            if j < 0 or j >= N_UNITS:
-                return
-            s = j % 2
-            wc, ws = state["w%d" % s]
+            wc, ws = state["w%d" % (j % 2)]
             xc, xs = state["x%d" % j]
-            bias8 = state["bias8"]
-            planar = pl_pool.tile([P, 4 * CHUNK], BF16)
             banks = []
             for t in range(4):
                 acc1 = ps_s1.tile([P, CHUNK], F32, tag="ps")
@@ -167,6 +191,15 @@ def tile_bispa_pa_t_kernel(
                     stop=True,
                 )
                 banks.append(acc1)
+            state["sb%d" % j] = banks
+
+        def s1_copies(j):
+            if not in_range(j):
+                return
+            s = j % 2
+            bias8 = state["bias8"]
+            banks = state["sb%d" % j]
+            planar = pl_pool.tile([P, 4 * CHUNK], BF16)
             for t in range(4):
                 dst = planar[:, t * CHUNK : (t + 1) * CHUNK]
                 b = bias8[:, 4 * s + t : 4 * s + t + 1]
@@ -177,7 +210,7 @@ def tile_bispa_pa_t_kernel(
             state["p%d" % j] = planar
 
         def regroup(j):
-            if j < 0 or j >= N_UNITS:
+            if not in_range(j):
                 return
             planar = state["p%d" % j]
             g2 = g2_pool.tile([P, 4 * CHUNK], BF16, align_bytes=64)
@@ -188,25 +221,20 @@ def tile_bispa_pa_t_kernel(
             state["g%d" % j] = g2
 
         def quantise2(j):
-            if j < 0 or j >= N_UNITS:
+            if not in_range(j):
                 return
             cc = cq.tile([P, CHUNK], U32, align_bytes=64)
             cs = cq.tile([P, CHUNK], U8, align_bytes=64)
             nc.vector.quantize_mx(out=cc[:].bitcast(FP8X4), scales=cs[:], in_=state["g%d" % j][:])
             state["c%d" % j] = (cc, cs)
 
-        def relu_tiles(q, on_scalar):
-            c = q // 2
-            tiles = (0, 1) if q % 2 == 0 else (2, 3)
-            return [a - tiles[0] for a in tiles if (c >= RELU_S_FROM or a >= 4 - RELU_S_TILES) == on_scalar]
+        def relu_on_scalar(q):
+            return q % 2 == 1 or q // 2 >= RELU_S_FROM
 
-        def stage2(q):
-            if q < 0 or q >= N_UNITS:
+        def s2_passes(q):
+            if not in_range(q):
                 return
             c = q // 2
-            ob = ob_pool.tile([P, 2 * E], F32)
-            state["o%d" % q] = ob
-            b1_bc = state["b1_bc"]
             banks = []
             for i in range(2):
                 a = 2 * (q % 2) + i
@@ -224,51 +252,69 @@ def tile_bispa_pa_t_kernel(
                         stop=(g == 1),
                     )
                 banks.append(acc2)
+            state["ab%d" % q] = banks
+
+        def s2_adds(q):
+            if not in_range(q):
+                return
+            ob = ob_pool.tile([P, 2 * E], F32)
+            state["o%d" % q] = ob
             for i in range(2):
                 nc.vector.tensor_tensor(
-                    out=ob[:, i * E : (i + 1) * E], in0=banks[i][:], in1=b1_bc[:], op=ALU.add
+                    out=ob[:, i * E : (i + 1) * E], in0=state["ab%d" % q][i][:], in1=state["b1_bc"][:], op=ALU.add
                 )
 
         def relu_vector(q):
-            if q < 0 or q >= N_UNITS:
-                return
-            mine = relu_tiles(q, False)
-            if mine:
-                span = state["o%d" % q][:, mine[0] * E : (mine[-1] + 1) * E]
-                nc.vector.tensor_scalar_max(out=span, in0=span, scalar1=0.0)
+            if in_range(q) and not relu_on_scalar(q):
+                ob = state["o%d" % q]
+                nc.vector.tensor_scalar_max(out=ob[:], in0=ob[:], scalar1=0.0)
 
         def relu_scalar_and_store(q):
-            if q < 0 or q >= N_UNITS:
+            if not in_range(q):
                 return
             c = q // 2
             ob = state["o%d" % q]
             rows = of[c * CHUNK : (c + 1) * CHUNK, :].rearrange("(p a) f -> p a f", a=4)
             first = 2 * (q % 2)
-            mine = relu_tiles(q, True)
-            for i in mine:
-                span = ob[:, i * E : (i + 1) * E]
-                nc.scalar.activation(out=span, in_=span, func=ACT.Relu)
-                if len(mine) == 2:
+            if relu_on_scalar(q):
+                for i in range(2):
+                    span = ob[:, i * E : (i + 1) * E]
+                    nc.scalar.activation(out=span, in_=span, func=ACT.Relu)
                     nc.sync.dma_start(out=rows[:, first + i, :], in_=span)
-            if len(mine) < 2:
+            else:
                 nc.sync.dma_start(
                     out=rows[:, first : first + 2, :], in_=ob[:].rearrange("p (a f) -> p a f", a=2)
                 )
 
         prepare_biases()
-        state["w0"] = weight_unit(hw_raw[:].bitcast(F32), 256, 0, "hw", True)
-        tq(0)
-        state["w1"] = weight_unit(vw_raw[:].bitcast(F32), 256, 0, "vw", True)
-        tq(1)
-        for m in range(N_UNITS + S2_LAG + 1):
-            stage1(m)
-            regroup(m)
+        for key, j in (("w0", 0), ("w1", 1)):
+            w_transposes(key)
+            w_copies(key)
+            w_quantise(key)
+            x_transposes(j)
+            x_copies(j)
+            x_quantise(j)
+        w_transposes("m0")
+        w_copies("m0")
+        w_quantise("m0")
+        x_transposes(2)
+        x_copies(2)
+
+        for m in range(N_UNITS + 6):
+            s1_passes(m)
             if m == 0:
-                state["m0"] = weight_unit(w1_raw[:].bitcast(F32), 512, 0, "w1a", False)
-            if m == 1:
-                state["m1"] = weight_unit(w1_raw[:].bitcast(F32), 512, 256, "w1b", False)
-            tq(m + 2)
-            quantise2(m)
-            relu_scalar_and_store(m - S2_LAG - 1)
-            stage2(m - S2_LAG)
-            relu_vector(m - S2_LAG)
+                w_transposes("m1")
+            x_transposes(m + 3)
+            s2_passes(m - 3)
+            s1_copies(m)
+            if m == 0:
+                w_copies("m1")
+            x_copies(m + 3)
+            relu_scalar_and_store(m - 5)
+            s2_adds(m - 4)
+            regroup(m - 1)
+            relu_vector(m - 4)
+            if m == 0:
+                w_quantise("m1")
+            x_quantise(m + 2)
+            quantise2(m - 1)

from contextlib import ExitStack

import concourse.mybir as mybir
from concourse.masks import make_identity

F32 = mybir.dt.float32
BF16 = mybir.dt.bfloat16
U32 = mybir.dt.uint32
U8 = mybir.dt.uint8
FP8X4 = mybir.dt.float8_e4m3fn_x4
ACT = mybir.ActivationFunctionType
ALU = mybir.AluOpType

P = 128
E = 512
CHUNK = 512
N_CHUNKS = 8
N_UNITS = 2 * N_CHUNKS
FLOPS = 2 * 4096 * 512 * 512 * 2 + 2 * 4096 * 1024 * 512

PINNED = True
XT_V_BELOW = 2
X1_V_BELOW = 2
RELU_S_FROM = 6
RELU_S_TILES = 2
S2_LAG = 2


def tile_bispa_pa_t_kernel(
    tc, h_ctx, v_ctx, h_out_w, h_out_b, v_out_w, v_out_b, mlp_w1, mlp_b1, out
):
    nc = tc.nc
    with ExitStack() as ctx:
        consts = ctx.enter_context(tc.tile_pool(name="consts", bufs=1))
        raw = ctx.enter_context(tc.tile_pool(name="raw", bufs=1))
        wq = ctx.enter_context(tc.tile_pool(name="wq", bufs=1))
        grp_pool = ctx.enter_context(tc.tile_pool(name="grp", bufs=3))
        xq = ctx.enter_context(tc.tile_pool(name="xq", bufs=5))
        pl_pool = ctx.enter_context(tc.tile_pool(name="pl", bufs=3))
        g2_pool = ctx.enter_context(tc.tile_pool(name="g2", bufs=3))
        cq = ctx.enter_context(tc.tile_pool(name="cq", bufs=7))
        ob_pool = ctx.enter_context(tc.tile_pool(name="ob", bufs=4))
        ps_tp = ctx.enter_context(tc.psum_pool(name="ps", bufs=8))
        ps_s1 = ps_tp
        ps_s2 = ps_tp
        if PINNED:
            ctx.enter_context(tc.manual_schedule())

        hx = h_ctx.flatten_outer_dims()
        vx = v_ctx.flatten_outer_dims()
        of = out.flatten_outer_dims()

        zb = consts.tile([P, 2 * P], BF16, name="zb")
        nc.vector.memset(zb[:], 0.0)
        zrow = consts.tile([P, E], BF16, name="zrow")
        nc.vector.memset(zrow[:], 0.0)
        ones = consts.tile([P, P], BF16, name="ones")
        nc.vector.memset(ones[:], 1.0)
        ident = consts.tile([P, P], F32, name="ident")
        make_identity(nc, ident[:])
        nc.sync.dma_start(out=zb[0:2, :], in_=h_out_b.rearrange("(u w) -> u w", u=2))
        nc.sync.dma_start(out=zb[2:4, :], in_=v_out_b.rearrange("(u w) -> u w", u=2))
        nc.sync.dma_start(out=zrow[0:1, :], in_=mlp_b1.rearrange("(o n) -> o n", o=1))

        def load_proj(w, name):
            t = raw.tile([P, 4 * E], BF16, name=name)
            nc.sync.dma_start(
                out=t[:].rearrange("q (u e k) -> q u e k", u=2, e=2),
                in_=w.rearrange("(u q e) k -> q u e k", u=2, e=2),
            )
            return t

        def load_ctx(x, c, name):
            t = raw.tile([P, 4 * E], BF16, name=name)
            nc.sync.dma_start(
                out=t[:].rearrange("p (a k) -> p a k", a=4),
                in_=x[c * CHUNK : (c + 1) * CHUNK, :].rearrange("(p a) k -> p a k", a=4),
            )
            return t

        ctx_raw = {}
        hw_raw = load_proj(h_out_w, "hw_raw")
        ctx_raw[0] = load_ctx(hx, 0, "x0")
        vw_raw = load_proj(v_out_w, "vw_raw")
        ctx_raw[1] = load_ctx(vx, 0, "x1")
        w1_raw = raw.tile([P, 4 * 2 * E], BF16, name="w1_raw")
        nc.sync.dma_start(
            out=w1_raw[:].rearrange("p (j k) -> p j k", j=4),
            in_=mlp_w1.rearrange("(j p) k -> p j k", p=P),
        )
        for c in range(1, N_CHUNKS):
            ctx_raw[2 * c] = load_ctx(hx, c, "x%d" % (2 * c))
            ctx_raw[2 * c + 1] = load_ctx(vx, c, "x%d" % (2 * c + 1))

        state = {}

        def in_range(j):
            return 0 <= j < N_UNITS

        def transposes(key, words, row_words, first_word):
            banks = []
            for half in range(2):
                bank = ps_tp.tile([P, E], F32, tag="ps")
                for jj in range(2):
                    for u in range(2):
                        start = (2 * half + jj) * row_words + first_word + u * P
                        nc.tensor.transpose(
                            bank[:, u * 256 + jj * P : u * 256 + (jj + 1) * P],
                            words[:, start : start + P],
                            ident[:],
                        )
                banks.append(bank)
            state["tb" + key] = banks

        def copies_out(key, second_on_vector):
            grp = grp_pool.tile([P, 4 * E], BF16, align_bytes=64)
            grp_words = grp[:].bitcast(F32)
            for half in range(2):
                dst = grp_words[:, half * E : (half + 1) * E].rearrange("p (r u) -> p r u", u=2)
                src = state["tb" + key][half][:].rearrange("p (u r) -> p r u", u=2)
                if second_on_vector and half == 1:
                    nc.vector.tensor_copy(out=dst, in_=src)
                else:
                    nc.scalar.copy(out=dst, in_=src)
            state["gr" + key] = grp

        def quantise(key, codes, scales):
            nc.vector.quantize_mx(out=codes[:].bitcast(FP8X4), scales=scales[:], in_=state["gr" + key][:])
            state[key] = (codes, scales)

        WEIGHTS = {
            "w0": (hw_raw, 256, 0, True),
            "w1": (vw_raw, 256, 0, True),
            "m0": (w1_raw, 512, 0, False),
            "m1": (w1_raw, 512, 256, False),
        }

        def w_transposes(key):
            tile_, row_words, first_word, on_v = WEIGHTS[key]
            transposes(key, tile_[:].bitcast(F32), row_words, first_word)

        def w_copies(key):
            copies_out(key, WEIGHTS[key][3])

        def w_quantise(key):
            codes = wq.tile([P, E], U32, name=key + "_c", align_bytes=64)
            scales = wq.tile([P, E], U8, name=key + "_s", align_bytes=64)
            quantise(key, codes, scales)

        def x_transposes(j):
            if in_range(j):
                transposes("x%d" % j, ctx_raw[j][:].bitcast(F32), 256, 0)

        def x_copies(j):
            if in_range(j):
                copies_out("x%d" % j, j < XT_V_BELOW)

        def x_quantise(j):
            if in_range(j):
                xc = xq.tile([P, E], U32, align_bytes=64)
                xs = xq.tile([P, E], U8, align_bytes=64)
                quantise("x%d" % j, xc, xs)

        def prepare_biases():
            bank = ps_tp.tile([P, E], F32, tag="ps")
            nc.tensor.transpose(bank[:, 0:P], zb[:].bitcast(F32), ident[:])
            bias8 = consts.tile([P, 8], F32, name="bias8")
            nc.vector.tensor_copy(out=bias8[:], in_=bank[:].bitcast(BF16)[:, 0:8])
            state["bias8"] = bias8
            acc = ps_s2.tile([P, E], F32, tag="ps")
            nc.tensor.matmul(out=acc[:], lhsT=ones[:], rhs=zrow[:], start=True, stop=True)
            b1_bc = consts.tile([P, E], F32, name="b1_bc")
            nc.vector.tensor_copy(out=b1_bc[:], in_=acc[:])
            state["b1_bc"] = b1_bc

        def s1_passes(j):
            if not in_range(j):
                return
            wc, ws = state["w%d" % (j % 2)]
            xc, xs = state["x%d" % j]
            banks = []
            for t in range(4):
                acc1 = ps_s1.tile([P, CHUNK], F32, tag="ps")
                nc.tensor.matmul_mx(
                    out=acc1[:],
                    lhsT=wc[:, t * P : (t + 1) * P].bitcast(FP8X4),
                    lhsT_scale=ws[:, t * P : (t + 1) * P],
                    rhs=xc[:].bitcast(FP8X4),
                    rhs_scale=xs[:],
                    start=True,
                    stop=True,
                )
                banks.append(acc1)
            state["sb%d" % j] = banks

        def s1_copies(j):
            if not in_range(j):
                return
            s = j % 2
            bias8 = state["bias8"]
            banks = state["sb%d" % j]
            planar = pl_pool.tile([P, 4 * CHUNK], BF16)
            for t in range(4):
                dst = planar[:, t * CHUNK : (t + 1) * CHUNK]
                b = bias8[:, 4 * s + t : 4 * s + t + 1]
                if j < X1_V_BELOW and t % 2 == 1:
                    nc.vector.tensor_scalar_add(out=dst, in0=banks[t][:], scalar1=b)
                else:
                    nc.scalar.activation(out=dst, in_=banks[t][:], func=ACT.Identity, bias=b, scale=1.0)
            state["p%d" % j] = planar

        def regroup(j):
            if not in_range(j):
                return
            planar = state["p%d" % j]
            g2 = g2_pool.tile([P, 4 * CHUNK], BF16, align_bytes=64)
            nc.vector.tensor_copy(
                out=g2[:].rearrange("p (c i t) -> p c t i", i=4, t=4),
                in_=planar[:].rearrange("p (t c i) -> p c t i", t=4, i=4),
            )
            state["g%d" % j] = g2

        def quantise2(j):
            if not in_range(j):
                return
            cc = cq.tile([P, CHUNK], U32, align_bytes=64)
            cs = cq.tile([P, CHUNK], U8, align_bytes=64)
            nc.vector.quantize_mx(out=cc[:].bitcast(FP8X4), scales=cs[:], in_=state["g%d" % j][:])
            state["c%d" % j] = (cc, cs)

        def relu_on_scalar(q):
            return q % 2 == 1 or q // 2 >= RELU_S_FROM

        def s2_passes(q):
            if not in_range(q):
                return
            c = q // 2
            banks = []
            for i in range(2):
                a = 2 * (q % 2) + i
                acc2 = ps_s2.tile([P, E], F32, tag="ps")
                for g in range(2):
                    cc, cs = state["c%d" % (2 * c + g)]
                    mc, ms = state["m%d" % g]
                    nc.tensor.matmul_mx(
                        out=acc2[:],
                        lhsT=cc[:, a * P : (a + 1) * P].bitcast(FP8X4),
                        lhsT_scale=cs[:, a * P : (a + 1) * P],
                        rhs=mc[:].bitcast(FP8X4),
                        rhs_scale=ms[:],
                        start=(g == 0),
                        stop=(g == 1),
                    )
                banks.append(acc2)
            state["ab%d" % q] = banks

        def s2_adds(q):
            if not in_range(q):
                return
            ob = ob_pool.tile([P, 2 * E], F32)
            state["o%d" % q] = ob
            for i in range(2):
                nc.vector.tensor_tensor(
                    out=ob[:, i * E : (i + 1) * E], in0=state["ab%d" % q][i][:], in1=state["b1_bc"][:], op=ALU.add
                )

        def relu_vector(q):
            if in_range(q) and not relu_on_scalar(q):
                ob = state["o%d" % q]
                nc.vector.tensor_scalar_max(out=ob[:], in0=ob[:], scalar1=0.0)

        def relu_scalar_and_store(q):
            if not in_range(q):
                return
            c = q // 2
            ob = state["o%d" % q]
            rows = of[c * CHUNK : (c + 1) * CHUNK, :].rearrange("(p a) f -> p a f", a=4)
            first = 2 * (q % 2)
            if relu_on_scalar(q):
                for i in range(2):
                    span = ob[:, i * E : (i + 1) * E]
                    nc.scalar.activation(out=span, in_=span, func=ACT.Relu)
                    nc.sync.dma_start(out=rows[:, first + i, :], in_=span)
            else:
                nc.sync.dma_start(
                    out=rows[:, first : first + 2, :], in_=ob[:].rearrange("p (a f) -> p a f", a=2)
                )

        prepare_biases()
        for key, j in (("w0", 0), ("w1", 1)):
            w_transposes(key)
            w_copies(key)
            w_quantise(key)
            x_transposes(j)
            x_copies(j)
            x_quantise(j)
        w_transposes("m0")
        w_copies("m0")
        w_quantise("m0")
        x_transposes(2)
        x_copies(2)

        for m in range(N_UNITS + 6):
            s1_passes(m)
            if m == 0:
                w_transposes("m1")
            x_transposes(m + 3)
            s2_passes(m - 3)
            s1_copies(m)
            if m == 0:
                w_copies("m1")
            x_copies(m + 3)
            relu_scalar_and_store(m - 5)
            s2_adds(m - 4)
            regroup(m - 1)
            relu_vector(m - 4)
            if m == 0:
                w_quantise("m1")
            x_quantise(m + 2)
            quantise2(m - 1)
